import numpy as np
import ml_dtypes


def mxq(x, axis, fmt="e4m3"):
    dtype, down = {"e4m3": (ml_dtypes.float8_e4m3fn, 7), "e5m2": (ml_dtypes.float8_e5m2, 14)}[fmt]
    v = np.moveaxis(np.asarray(x, np.float32).astype(ml_dtypes.bfloat16).astype(np.float64), axis, -1)
    blocks = v.reshape(v.shape[:-1] + (-1, 32))
    amax = np.abs(blocks).max(-1, keepdims=True)
    byte = np.maximum(np.where(amax > 0, np.frexp(amax)[1] - 1 + 127, 0) - down, 1)
    scale = np.exp2(byte - 127.0)
    codes = (blocks / scale).astype(np.float32).astype(dtype).astype(np.float64)
    return np.moveaxis((codes * scale).reshape(v.shape), -1, axis)


WIDE = False


def mx_kscale(k):
    if not WIDE:
        return np.ones(k)
    levels = np.array([10, -10, 5, -5, 0])
    if k % 512:
        return np.exp2(np.random.permutation(np.resize(levels, k // 32))).repeat(32)
    a = np.empty((k // 512, 16))
    for p in range(k // 512):
        a[p, :8] = np.random.permutation(np.resize(levels, 8))
        for g in range(8):
            far = levels[np.abs(levels - a[p, g]) >= 10]
            a[p, g + 8] = far[np.random.randint(len(far))]
    return np.exp2(a.ravel()).repeat(32)


BF16 = ml_dtypes.bfloat16


def bf(x):
    return np.asarray(x, np.float32).astype(BF16)


def f64(x):
    return np.asarray(x).astype(np.float64)


B, S, H, O, W = 8, 2048, 512, 128, 8


def draw0():
    s = mx_kscale(H)
    return {"hidden_states": bf(np.random.standard_normal((B, S, H)) * s),
            "gate_proj": bf(np.random.standard_normal((O, H)) / np.sqrt(H) / s[None, :]),
            "world_size": W}


def core(hidden_states, gate_proj, world_size):
    h = gate_proj.shape[1]
    view = f64(hidden_states).reshape(-1, h)
    mm = mxq(view, 1, "e4m3") @ mxq(f64(gate_proj), 1, "e4m3").T
    n, o = mm.shape
    out = mm.reshape(world_size, n // world_size, o).sum(axis=0)
    return out


def e4m3fn_bytes(y):
    return np.clip(np.asarray(y, np.float64), -448.0, 448.0).astype(np.float32).astype(ml_dtypes.float8_e4m3fn).view(np.uint8)


def e4m3fn_values(b):
    return np.asarray(b, np.uint8).view(ml_dtypes.float8_e4m3fn).astype(np.float64)


def setup_inputs():
    d = draw0()
    x0 = np.asarray(d['hidden_states']).astype(np.float64)
    s = (np.max(np.abs(x0), axis=(0, 1), keepdims=True) / 448.0).astype(np.float32)
    out = {}
    for k, v in d.items():
        if k == 'hidden_states':
            out['hidden_states_bytes'] = e4m3fn_bytes(x0 / s.astype(np.float64))
            out['hidden_states_scale'] = s
        else:
            out[k] = v
    return out


def reference(hidden_states_bytes, hidden_states_scale, gate_proj, world_size):
    return core(e4m3fn_values(hidden_states_bytes) * hidden_states_scale.astype(np.float64), gate_proj, world_size)

@@ -1,0 +1,240 @@
+from contextlib import ExitStack
+
+import concourse.mybir as mybir
+from concourse.masks import make_identity
+
+F32 = mybir.dt.float32
+BF16 = mybir.dt.bfloat16
+U32 = mybir.dt.uint32
+U8 = mybir.dt.uint8
+FP8 = mybir.dt.float8_e4m3fn
+FP8X4 = mybir.dt.float8_e4m3fn_x4
+
+P = 128
+CHUNKS = 8
+ROWS = 2048
+K = 512
+OUT = 128
+SLOTS = ROWS // P
+PACK = 4
+WORDS = K // 2
+BANK_SLOTS = 4
+
+FIRST_PART = 4
+SCALAR_UNITS = 2
+UNIT_BY_UNIT_SLOTS = 2
+LAST_PIECES = [4, 2, 2]
+
+FLOPS = 2 * CHUNKS * ROWS * K * OUT
+
+
+def scalar_takes_part(i):
+    return 0 <= i < SLOTS and i % 4 != 3
+
+
+def vector_units(i):
+    return CHUNKS - SCALAR_UNITS if scalar_takes_part(i) else CHUNKS
+
+
+def is_slot(i):
+    return 0 <= i < SLOTS
+
+
+def tile_testmmrsmodel_t_kernel(tc, hidden_states_bytes, hidden_states_scale, gate_proj, world_size, out):
+    nc = tc.nc
+    assert world_size == CHUNKS
+
+    bytes_by_slot = hidden_states_bytes.rearrange("r (p i) k -> i p r k", i=SLOTS)
+    out_by_slot = out.rearrange("(p i) o -> p i o", i=SLOTS)
+
+    with ExitStack() as ctx:
+        ctx.enter_context(tc.manual_schedule())
+        keep = ctx.enter_context(tc.tile_pool(name="keep", bufs=1))
+        short = ctx.enter_context(tc.tile_pool(name="short", bufs=3))
+        grouped_pool = ctx.enter_context(tc.tile_pool(name="grouped_pool", bufs=4))
+        turned_pool = ctx.enter_context(tc.psum_pool(name="turned_pool", bufs=6))
+        sums_pool = ctx.enter_context(tc.psum_pool(name="sums_pool", bufs=2))
+
+        scale_rows = keep.tile([P, FIRST_PART * K], F32, name="scale_rows")
+        nc.sync.dma_start(out=scale_rows[:, 0:K], in_=hidden_states_scale.rearrange("a b k -> (a b k)").partition_broadcast(P))
+        w_rows = keep.tile([P, K], BF16, name="w_rows")
+        nc.scalar.dma_start(out=w_rows[:], in_=gate_proj)
+        scale_cols = keep.tile([P, PACK], F32, name="scale_cols")
+        nc.scalar.dma_start(out=scale_cols[:], in_=hidden_states_scale.rearrange("a b (p t) -> p (a b t)", t=PACK))
+        x_bytes = []
+        for i in range(SLOTS):
+            slot_bytes = keep.tile([P, CHUNKS, K], U8, name="x_bytes%d" % i)
+            units = 2 if i == 0 else 4
+            for r in range(0, CHUNKS, units):
+                nc.sync.dma_start(out=slot_bytes[:, r : r + units, :], in_=bytes_by_slot[i][:, r : r + units, :])
+            x_bytes.append(slot_bytes)
+            if i == UNIT_BY_UNIT_SLOTS - 1:
+                for replica in range(1, FIRST_PART):
+                    nc.sync.dma_start(out=scale_rows[:, replica * K : (replica + 1) * K], in_=scale_rows[:, 0:K])
+
+        ident = keep.tile([P, P], F32, name="ident")
+        make_identity(nc, ident[:])
+        warm_in = keep.tile([P, 1], F32, name="warm_in")
+        warm_out = keep.tile([P, 1], F32, name="warm_out")
+        nc.gpsimd.memset(warm_in[:], 0.0)
+        nc.scalar.copy(out=warm_out[:], in_=warm_in[:])
+
+        w_grouped = keep.tile([P, K], BF16, name="w_grouped", align_bytes=64)
+        w_codes = keep.tile([P, OUT], U32, name="w_codes", align_bytes=64)
+        w_block_scales = keep.tile([P, OUT], U8, name="w_block_scales", align_bytes=64)
+
+        scaled = {}
+        widened = {}
+        widened_turned = {}
+        planes = {}
+        grouped = {}
+        codes = {}
+        block_scales = {}
+        sums = {}
+
+        def as_fp8(i):
+            return x_bytes[i][:].rearrange("p r k -> p (r k)").bitcast(FP8)
+
+        def grouped_of(i):
+            if i not in grouped:
+                new_grouped = grouped_pool.tile([P, CHUNKS * K], BF16, name="grouped_tile", align_bytes=64)
+                grouped[i] = new_grouped
+            return grouped[i]
+
+        def part_units(i, part):
+            return (0, FIRST_PART) if part == 0 else (FIRST_PART, vector_units(i))
+
+        def vector_product(i, part):
+            if part == 0:
+                new_scaled = short.tile([P, CHUNKS * K], BF16, name="scaled_tile")
+                scaled[i] = new_scaled
+            first, end = part_units(i, part)
+            width = 1 if i < UNIT_BY_UNIT_SLOTS else end - first
+            for unit in range(first, end, width):
+                cols = slice(unit * K, (unit + width) * K)
+                nc.vector.tensor_tensor(
+                    out=scaled[i][:, cols], in0=as_fp8(i)[:, cols], in1=scale_rows[:, 0 : width * K], op=mybir.AluOpType.mult
+                )
+
+        def turn_two_units(rows, first_unit):
+            words = rows.bitcast(F32)
+            bank = turned_pool.tile([P, 2, 2, P], F32, name="bank")
+            for n in range(2):
+                word0 = WORDS * (first_unit + n)
+                for u in range(2):
+                    nc.tensor.transpose(bank[:, n, u, :], words[:, word0 + u : word0 + WORDS : 2], ident[:])
+            return bank
+
+        def turn_vector_units(i, part):
+            first, end = part_units(i, part)
+            for unit in range(first, end, 2):
+                bank = turn_two_units(scaled[i][:], unit)
+                nc.scalar.copy(
+                    out=grouped_of(i)[:, unit * K : (unit + 2) * K].bitcast(F32).rearrange("p (n c u) -> p n c u", n=2, u=2),
+                    in_=bank[:].rearrange("p n u c -> p n c u"),
+                )
+
+        def scalar_widen(i):
+            new_widened = short.tile([P, SCALAR_UNITS * K], BF16, name="widened_tile")
+            widened[i] = new_widened
+            nc.scalar.copy(out=new_widened[:], in_=as_fp8(i)[:, vector_units(i) * K : CHUNKS * K])
+
+        def scalar_turn(i):
+            widened_turned[i] = turn_two_units(widened[i][:], 0)
+
+        def scalar_product(i):
+            new_planes = short.tile([P, PACK, SCALAR_UNITS * P], BF16, name="planes_tile")
+            planes[i] = new_planes
+            halves = widened_turned[i][:].rearrange("p n u c -> p (n u c)").bitcast(BF16)
+            halves = halves.rearrange("p (n u c e) -> p n u c e", n=2, u=2, e=2)
+            for t in range(PACK):
+                nc.scalar.activation(
+                    out=new_planes[:, t, :].rearrange("p (n c) -> p n c", n=2),
+                    in_=halves[:, :, t // 2, :, t % 2],
+                    func=mybir.ActivationFunctionType.Copy,
+                    scale=scale_cols[:, t : t + 1],
+                )
+
+        def scalar_weave(i):
+            nc.scalar.copy(
+                out=grouped_of(i)[:, vector_units(i) * K : CHUNKS * K].rearrange("p (c t) -> p c t", t=PACK),
+                in_=planes[i][:].rearrange("p t c -> p c t"),
+            )
+
+        def quantize(i, first, end):
+            if first == 0:
+                new_codes = short.tile([P, CHUNKS * P], U32, name="codes_tile", align_bytes=64)
+                new_block_scales = short.tile([P, CHUNKS * P], U8, name="block_scales_tile", align_bytes=64)
+                codes[i] = new_codes
+                block_scales[i] = new_block_scales
+            nc.vector.quantize_mx(
+                out=codes[i][:, first * P : end * P].bitcast(FP8X4),
+                scales=block_scales[i][:, first * P : end * P],
+                in_=grouped[i][:, first * K : end * K],
+            )
+
+        def store(first_slot, n_slots):
+            place = first_slot % BANK_SLOTS
+            result = short.tile([P, BANK_SLOTS, OUT], F32, name="result")
+            nc.scalar.copy(out=result[:, 0:n_slots, :], in_=sums[first_slot // BANK_SLOTS][:, place : place + n_slots, :])
+            nc.sync.dma_start(out=out_by_slot[:, first_slot : first_slot + n_slots, :], in_=result[:, 0:n_slots, :])
+
+        def multiply(i, first, end):
+            if i % BANK_SLOTS == 0 and first == 0:
+                new_sums = sums_pool.tile([P, BANK_SLOTS, OUT], F32, name="sums_tile")
+                sums[i // BANK_SLOTS] = new_sums
+            for r in range(first, end):
+                cols = slice(r * P, (r + 1) * P)
+                nc.tensor.matmul_mx(
+                    out=sums[i // BANK_SLOTS][:, i % BANK_SLOTS, :],
+                    lhsT=codes[i][:, cols].bitcast(FP8X4),
+                    lhsT_scale=block_scales[i][:, cols],
+                    rhs=w_codes[:].bitcast(FP8X4),
+                    rhs_scale=w_block_scales[:],
+                    start=(r == 0),
+                    stop=(r == CHUNKS - 1),
+                )
+            if end == CHUNKS:
+                if i == SLOTS - 2:
+                    store(i - 2, BANK_SLOTS - 1)
+                elif i == SLOTS - 1:
+                    store(i, 1)
+                elif i % BANK_SLOTS == BANK_SLOTS - 1:
+                    store(i - BANK_SLOTS + 1, BANK_SLOTS)
+
+        w_words = w_rows[:].bitcast(F32)
+        w_bank = turned_pool.tile([P, 2, 2, P], F32, name="bank")
+        for u in range(2):
+            nc.tensor.transpose(w_bank[:, 0, u, :], w_words[:, u:WORDS:2], ident[:])
+        nc.scalar.copy(
+            out=w_grouped[:].bitcast(F32).rearrange("p (c u) -> p c u", u=2),
+            in_=w_bank[:, 0, :, :].rearrange("p u c -> p c u"),
+        )
+
+        for step in range(-1, SLOTS + 2):
+            if is_slot(step):
+                vector_product(step, 0)
+            if step == 1:
+                nc.vector.quantize_mx(out=w_codes[:].bitcast(FP8X4), scales=w_block_scales[:], in_=w_grouped[:])
+            if is_slot(step - 1):
+                turn_vector_units(step - 1, 1)
+            if scalar_takes_part(step - 1):
+                scalar_weave(step - 1)
+            if step - 2 == SLOTS - 1:
+                first = 0
+                for n_units in LAST_PIECES:
+                    quantize(step - 2, first, first + n_units)
+                    multiply(step - 2, first, first + n_units)
+                    first += n_units
+            elif is_slot(step - 2):
+                quantize(step - 2, 0, CHUNKS)
+            if is_slot(step):
+                vector_product(step, 1)
+                turn_vector_units(step, 0)
+            if scalar_takes_part(step):
+                scalar_turn(step)
+                scalar_product(step)
+            if scalar_takes_part(step + 1):
+                scalar_widen(step + 1)
+            if is_slot(step - 2) and step - 2 != SLOTS - 1:
+                multiply(step - 2, 0, CHUNKS)

@@ -29,7 +29,7 @@ FLOPS = 2 * CHUNKS * ROWS * K * OUT
 
 
 def scalar_takes_part(i):
-    return 0 <= i < SLOTS and i % 4 != 3
+    return 0 <= i < SLOTS and i % 8 != 7
 
 
 def vector_units(i):

@@ -29,7 +29,7 @@ FLOPS = 2 * CHUNKS * ROWS * K * OUT
 
 
 def scalar_takes_part(i):
-    return 0 <= i < SLOTS and i % 8 != 7
+    return 0 <= i < SLOTS
 
 
 def vector_units(i):

@@ -19,25 +19,25 @@ SLOTS = ROWS // P
 PACK = 4
 WORDS = K // 2
 BANK_SLOTS = 4
-
-FIRST_PART = 4
-SCALAR_UNITS = 2
-UNIT_BY_UNIT_SLOTS = 2
+PAIRS = CHUNKS // 2
+PAIR_COLS = 2 * P
 LAST_PIECES = [4, 2, 2]
+
+WEAVE_ON_GPSIMD = False
 
 FLOPS = 2 * CHUNKS * ROWS * K * OUT
 
 
-def scalar_takes_part(i):
-    return 0 <= i < SLOTS
-
-
-def vector_units(i):
-    return CHUNKS - SCALAR_UNITS if scalar_takes_part(i) else CHUNKS
-
-
 def is_slot(i):
     return 0 <= i < SLOTS
+
+
+def scalar_pairs(i):
+    return 1
+
+
+def scalar_widens(i):
+    return 3
 
 
 def tile_testmmrsmodel_t_kernel(tc, hidden_states_bytes, hidden_states_scale, gate_proj, world_size, out):
@@ -51,16 +51,14 @@ def tile_testmmrsmodel_t_kernel(tc, hidden_states_bytes, hidden_states_scale, ga
         ctx.enter_context(tc.manual_schedule())
         keep = ctx.enter_context(tc.tile_pool(name="keep", bufs=1))
         short = ctx.enter_context(tc.tile_pool(name="short", bufs=3))
-        grouped_pool = ctx.enter_context(tc.tile_pool(name="grouped_pool", bufs=4))
+        rows_pool = ctx.enter_context(tc.tile_pool(name="rows_pool", bufs=3))
         turned_pool = ctx.enter_context(tc.psum_pool(name="turned_pool", bufs=6))
         sums_pool = ctx.enter_context(tc.psum_pool(name="sums_pool", bufs=2))
 
-        scale_rows = keep.tile([P, FIRST_PART * K], F32, name="scale_rows")
-        nc.sync.dma_start(out=scale_rows[:, 0:K], in_=hidden_states_scale.rearrange("a b k -> (a b k)").partition_broadcast(P))
         w_rows = keep.tile([P, K], BF16, name="w_rows")
-        nc.scalar.dma_start(out=w_rows[:], in_=gate_proj)
         scale_cols = keep.tile([P, PACK], F32, name="scale_cols")
         nc.scalar.dma_start(out=scale_cols[:], in_=hidden_states_scale.rearrange("a b (p t) -> p (a b t)", t=PACK))
+        nc.scalar.dma_start(out=w_rows[:], in_=gate_proj)
         x_bytes = []
         for i in range(SLOTS):
             slot_bytes = keep.tile([P, CHUNKS, K], U8, name="x_bytes%d" % i)
@@ -68,9 +66,6 @@ def tile_testmmrsmodel_t_kernel(tc, hidden_states_bytes, hidden_states_scale, ga
             for r in range(0, CHUNKS, units):
                 nc.sync.dma_start(out=slot_bytes[:, r : r + units, :], in_=bytes_by_slot[i][:, r : r + units, :])
             x_bytes.append(slot_bytes)
-            if i == UNIT_BY_UNIT_SLOTS - 1:
-                for replica in range(1, FIRST_PART):
-                    nc.sync.dma_start(out=scale_rows[:, replica * K : (replica + 1) * K], in_=scale_rows[:, 0:K])
 
         ident = keep.tile([P, P], F32, name="ident")
         make_identity(nc, ident[:])
@@ -79,13 +74,18 @@ def tile_testmmrsmodel_t_kernel(tc, hidden_states_bytes, hidden_states_scale, ga
         nc.gpsimd.memset(warm_in[:], 0.0)
         nc.scalar.copy(out=warm_out[:], in_=warm_in[:])
 
+        scale_pair = keep.tile([P, PAIR_COLS * PACK], F32, name="scale_pair")
+        nc.vector.tensor_copy(
+            out=scale_pair[:].rearrange("p (m t) -> p m t", t=PACK),
+            in_=scale_cols[:].unsqueeze(1).to_broadcast([P, PAIR_COLS, PACK]),
+        )
+
         w_grouped = keep.tile([P, K], BF16, name="w_grouped", align_bytes=64)
         w_codes = keep.tile([P, OUT], U32, name="w_codes", align_bytes=64)
         w_block_scales = keep.tile([P, OUT], U8, name="w_block_scales", align_bytes=64)
 
-        scaled = {}
         widened = {}
-        widened_turned = {}
+        banks = {}
         planes = {}
         grouped = {}
         codes = {}
@@ -97,69 +97,60 @@ def tile_testmmrsmodel_t_kernel(tc, hidden_states_bytes, hidden_states_scale, ga
 
         def grouped_of(i):
             if i not in grouped:
-                new_grouped = grouped_pool.tile([P, CHUNKS * K], BF16, name="grouped_tile", align_bytes=64)
+                new_grouped = rows_pool.tile([P, CHUNKS * K], BF16, name="rows_tile", align_bytes=64)
                 grouped[i] = new_grouped
             return grouped[i]
 
-        def part_units(i, part):
-            return (0, FIRST_PART) if part == 0 else (FIRST_PART, vector_units(i))
+        def pair_of_grouped(i, b):
+            return grouped_of(i)[:, 2 * b * K : (2 * b + 2) * K]
 
-        def vector_product(i, part):
-            if part == 0:
-                new_scaled = short.tile([P, CHUNKS * K], BF16, name="scaled_tile")
-                scaled[i] = new_scaled
-            first, end = part_units(i, part)
-            width = 1 if i < UNIT_BY_UNIT_SLOTS else end - first
-            for unit in range(first, end, width):
-                cols = slice(unit * K, (unit + width) * K)
-                nc.vector.tensor_tensor(
-                    out=scaled[i][:, cols], in0=as_fp8(i)[:, cols], in1=scale_rows[:, 0 : width * K], op=mybir.AluOpType.mult
-                )
+        def widen(engine_copy, i, first, end):
+            if i not in widened:
+                new_widened = rows_pool.tile([P, CHUNKS * K], BF16, name="rows_tile", align_bytes=64)
+                widened[i] = new_widened
+            engine_copy(out=widened[i][:, first * K : end * K], in_=as_fp8(i)[:, first * K : end * K])
 
-        def turn_two_units(rows, first_unit):
-            words = rows.bitcast(F32)
+        def turn(i, b):
+            words = widened[i][:].bitcast(F32)
             bank = turned_pool.tile([P, 2, 2, P], F32, name="bank")
             for n in range(2):
-                word0 = WORDS * (first_unit + n)
+                word0 = WORDS * (2 * b + n)
                 for u in range(2):
-                    nc.tensor.transpose(bank[:, n, u, :], words[:, word0 + u : word0 + WORDS : 2], ident[:])
-            return bank
+                    nc.tensor.transpose(bank[:, u, n, :], words[:, word0 + u : word0 + WORDS : 2], ident[:])
+            banks[(i, b)] = bank
 
-        def turn_vector_units(i, part):
-            first, end = part_units(i, part)
-            for unit in range(first, end, 2):
-                bank = turn_two_units(scaled[i][:], unit)
-                nc.scalar.copy(
-                    out=grouped_of(i)[:, unit * K : (unit + 2) * K].bitcast(F32).rearrange("p (n c u) -> p n c u", n=2, u=2),
-                    in_=bank[:].rearrange("p n u c -> p n c u"),
-                )
+        def halves_of(i, b):
+            return banks[(i, b)][:].rearrange("p u n c -> p (u n c)").bitcast(BF16)
 
-        def scalar_widen(i):
-            new_widened = short.tile([P, SCALAR_UNITS * K], BF16, name="widened_tile")
-            widened[i] = new_widened
-            nc.scalar.copy(out=new_widened[:], in_=as_fp8(i)[:, vector_units(i) * K : CHUNKS * K])
+        def vector_product(i, b):
+            nc.vector.tensor_tensor(
+                out=pair_of_grouped(i, b).rearrange("p (m u e) -> p m u e", u=2, e=2),
+                in0=halves_of(i, b).rearrange("p (u m e) -> p m u e", u=2, e=2),
+                in1=scale_pair[:].rearrange("p (m u e) -> p m u e", u=2, e=2),
+                op=mybir.AluOpType.mult,
+            )
 
-        def scalar_turn(i):
-            widened_turned[i] = turn_two_units(widened[i][:], 0)
-
-        def scalar_product(i):
-            new_planes = short.tile([P, PACK, SCALAR_UNITS * P], BF16, name="planes_tile")
-            planes[i] = new_planes
-            halves = widened_turned[i][:].rearrange("p n u c -> p (n u c)").bitcast(BF16)
-            halves = halves.rearrange("p (n u c e) -> p n u c e", n=2, u=2, e=2)
+        def scalar_product(i, b):
+            new_planes = short.tile([P, PACK, PAIR_COLS], BF16, name="planes_tile%d" % b)
+            planes[(i, b)] = new_planes
+            halves = halves_of(i, b).rearrange("p (u m e) -> p u m e", u=2, e=2)
             for t in range(PACK):
                 nc.scalar.activation(
-                    out=new_planes[:, t, :].rearrange("p (n c) -> p n c", n=2),
-                    in_=halves[:, :, t // 2, :, t % 2],
+                    out=new_planes[:, t, :],
+                    in_=halves[:, t // 2, :, t % 2],
                     func=mybir.ActivationFunctionType.Copy,
                     scale=scale_cols[:, t : t + 1],
                 )
 
-        def scalar_weave(i):
-            nc.scalar.copy(
-                out=grouped_of(i)[:, vector_units(i) * K : CHUNKS * K].rearrange("p (c t) -> p c t", t=PACK),
-                in_=planes[i][:].rearrange("p t c -> p c t"),
-            )
+        def weave(i, b):
+            woven = pair_of_grouped(i, b).rearrange("p (m t) -> p m t", t=PACK)
+            by_column = planes[(i, b)][:].rearrange("p t m -> p m t")
+            if WEAVE_ON_GPSIMD:
+                nc.gpsimd.tensor_scalar(
+                    out=woven, in0=by_column, scalar1=1.0, scalar2=0.0, op0=mybir.AluOpType.mult, op1=mybir.AluOpType.add
+                )
+            else:
+                nc.scalar.copy(out=woven, in_=by_column)
 
         def quantize(i, first, end):
             if first == 0:
@@ -194,47 +185,54 @@ def tile_testmmrsmodel_t_kernel(tc, hidden_states_bytes, hidden_states_scale, ga
                     start=(r == 0),
                     stop=(r == CHUNKS - 1),
                 )
-            if end == CHUNKS:
-                if i == SLOTS - 2:
-                    store(i - 2, BANK_SLOTS - 1)
-                elif i == SLOTS - 1:
-                    store(i, 1)
-                elif i % BANK_SLOTS == BANK_SLOTS - 1:
-                    store(i - BANK_SLOTS + 1, BANK_SLOTS)
 
-        w_words = w_rows[:].bitcast(F32)
-        w_bank = turned_pool.tile([P, 2, 2, P], F32, name="bank")
-        for u in range(2):
-            nc.tensor.transpose(w_bank[:, 0, u, :], w_words[:, u:WORDS:2], ident[:])
-        nc.scalar.copy(
-            out=w_grouped[:].bitcast(F32).rearrange("p (c u) -> p c u", u=2),
-            in_=w_bank[:, 0, :, :].rearrange("p u c -> p c u"),
-        )
+        def turn_gate_proj():
+            w_words = w_rows[:].bitcast(F32)
+            w_bank = turned_pool.tile([P, 2, 2, P], F32, name="bank")
+            for u in range(2):
+                nc.tensor.transpose(w_bank[:, u, 0, :], w_words[:, u:WORDS:2], ident[:])
+            nc.scalar.copy(
+                out=w_grouped[:].bitcast(F32).rearrange("p (c u) -> p c u", u=2),
+                in_=w_bank[:, :, 0, :].rearrange("p u c -> p c u"),
+            )
 
-        for step in range(-1, SLOTS + 2):
+        for step in range(-2, SLOTS + 2):
             if is_slot(step):
-                vector_product(step, 0)
-            if step == 1:
+                for b in range(scalar_pairs(step)):
+                    scalar_product(step, b)
+                vector_product(step, scalar_pairs(step))
+            if step == 0:
                 nc.vector.quantize_mx(out=w_codes[:].bitcast(FP8X4), scales=w_block_scales[:], in_=w_grouped[:])
-            if is_slot(step - 1):
-                turn_vector_units(step - 1, 1)
-            if scalar_takes_part(step - 1):
-                scalar_weave(step - 1)
-            if step - 2 == SLOTS - 1:
+            if is_slot(step - 1) and step - 1 != SLOTS - 1:
+                quantize(step - 1, 0, CHUNKS)
+            if is_slot(step):
+                for b in range(scalar_pairs(step) + 1, PAIRS):
+                    vector_product(step, b)
+                for b in range(scalar_pairs(step)):
+                    weave(step, b)
+            if is_slot(step - 2) and (step - 2) % BANK_SLOTS == BANK_SLOTS - 1 and step - 2 != SLOTS - 1:
+                store(step - 2 - (BANK_SLOTS - 1), BANK_SLOTS)
+            if step + 2 == 0:
+                widen(nc.scalar.copy, 0, 0, 2)
+                for b in range(1, PAIRS):
+                    widen(nc.vector.tensor_copy, 0, 2 * b, 2 * b + 2)
+                turn_gate_proj()
+            elif is_slot(step + 2):
+                split = scalar_widens(step + 2)
+                widen(nc.scalar.copy, step + 2, 0, split)
+                middle = (split + CHUNKS + 1) // 2
+                widen(nc.gpsimd.tensor_copy, step + 2, split, middle)
+                widen(nc.gpsimd.tensor_copy, step + 2, middle, CHUNKS)
+            if is_slot(step + 1):
+                for b in range(PAIRS):
+                    turn(step + 1, b)
+            if step - 1 == SLOTS - 1:
+                store(SLOTS - BANK_SLOTS, BANK_SLOTS - 1)
                 first = 0
                 for n_units in LAST_PIECES:
-                    quantize(step - 2, first, first + n_units)
-                    multiply(step - 2, first, first + n_units)
+                    quantize(step - 1, first, first + n_units)
+                    multiply(step - 1, first, first + n_units)
                     first += n_units
-            elif is_slot(step - 2):
-                quantize(step - 2, 0, CHUNKS)
-            if is_slot(step):
-                vector_product(step, 1)
-                turn_vector_units(step, 0)
-            if scalar_takes_part(step):
-                scalar_turn(step)
-                scalar_product(step)
-            if scalar_takes_part(step + 1):
-                scalar_widen(step + 1)
-            if is_slot(step - 2) and step - 2 != SLOTS - 1:
-                multiply(step - 2, 0, CHUNKS)
+                store(SLOTS - 1, 1)
+            elif is_slot(step - 1):
+                multiply(step - 1, 0, CHUNKS)

@@ -37,7 +37,7 @@ def scalar_pairs(i):
 
 
 def scalar_widens(i):
-    return 3
+    return 7 * K // 2
 
 
 def tile_testmmrsmodel_t_kernel(tc, hidden_states_bytes, hidden_states_scale, gate_proj, world_size, out):
@@ -104,11 +104,14 @@ def tile_testmmrsmodel_t_kernel(tc, hidden_states_bytes, hidden_states_scale, ga
         def pair_of_grouped(i, b):
             return grouped_of(i)[:, 2 * b * K : (2 * b + 2) * K]
 
-        def widen(engine_copy, i, first, end):
+        def widen_columns(engine_copy, i, first_col, end_col):
             if i not in widened:
                 new_widened = rows_pool.tile([P, CHUNKS * K], BF16, name="rows_tile", align_bytes=64)
                 widened[i] = new_widened
-            engine_copy(out=widened[i][:, first * K : end * K], in_=as_fp8(i)[:, first * K : end * K])
+            engine_copy(out=widened[i][:, first_col:end_col], in_=as_fp8(i)[:, first_col:end_col])
+
+        def widen(engine_copy, i, first, end):
+            widen_columns(engine_copy, i, first * K, end * K)
 
         def turn(i, b):
             words = widened[i][:].bitcast(F32)
@@ -219,10 +222,10 @@ def tile_testmmrsmodel_t_kernel(tc, hidden_states_bytes, hidden_states_scale, ga
                 turn_gate_proj()
             elif is_slot(step + 2):
                 split = scalar_widens(step + 2)
-                widen(nc.scalar.copy, step + 2, 0, split)
-                middle = (split + CHUNKS + 1) // 2
-                widen(nc.gpsimd.tensor_copy, step + 2, split, middle)
-                widen(nc.gpsimd.tensor_copy, step + 2, middle, CHUNKS)
+                widen_columns(nc.scalar.copy, step + 2, 0, split)
+                middle = (split + CHUNKS * K) // 2
+                widen_columns(nc.gpsimd.tensor_copy, step + 2, split, middle)
+                widen_columns(nc.gpsimd.tensor_copy, step + 2, middle, CHUNKS * K)
             if is_slot(step + 1):
                 for b in range(PAIRS):
                     turn(step + 1, b)

@@ -21,9 +21,9 @@ WORDS = K // 2
 BANK_SLOTS = 4
 PAIRS = CHUNKS // 2
 PAIR_COLS = 2 * P
-LAST_PIECES = [4, 2, 2]
+LAST_PIECES = [(4, 8), (0, 2), (2, 4)]
 
-WEAVE_ON_GPSIMD = False
+GPSIMD_WEAVES_PAIR = 1
 
 FLOPS = 2 * CHUNKS * ROWS * K * OUT
 
@@ -33,7 +33,7 @@ def is_slot(i):
 
 
 def scalar_pairs(i):
-    return 1
+    return 2 if i >= SLOTS - 2 else 1
 
 
 def scalar_widens(i):
@@ -148,7 +148,7 @@ def tile_testmmrsmodel_t_kernel(tc, hidden_states_bytes, hidden_states_scale, ga
         def weave(i, b):
             woven = pair_of_grouped(i, b).rearrange("p (m t) -> p m t", t=PACK)
             by_column = planes[(i, b)][:].rearrange("p t m -> p m t")
-            if WEAVE_ON_GPSIMD:
+            if b == GPSIMD_WEAVES_PAIR:
                 nc.gpsimd.tensor_scalar(
                     out=woven, in0=by_column, scalar1=1.0, scalar2=0.0, op0=mybir.AluOpType.mult, op1=mybir.AluOpType.add
                 )
@@ -156,7 +156,7 @@ def tile_testmmrsmodel_t_kernel(tc, hidden_states_bytes, hidden_states_scale, ga
                 nc.scalar.copy(out=woven, in_=by_column)
 
         def quantize(i, first, end):
-            if first == 0:
+            if i not in codes:
                 new_codes = short.tile([P, CHUNKS * P], U32, name="codes_tile", align_bytes=64)
                 new_block_scales = short.tile([P, CHUNKS * P], U8, name="block_scales_tile", align_bytes=64)
                 codes[i] = new_codes
@@ -173,8 +173,8 @@ def tile_testmmrsmodel_t_kernel(tc, hidden_states_bytes, hidden_states_scale, ga
             nc.scalar.copy(out=result[:, 0:n_slots, :], in_=sums[first_slot // BANK_SLOTS][:, place : place + n_slots, :])
             nc.sync.dma_start(out=out_by_slot[:, first_slot : first_slot + n_slots, :], in_=result[:, 0:n_slots, :])
 
-        def multiply(i, first, end):
-            if i % BANK_SLOTS == 0 and first == 0:
+        def multiply(i, first, end, opens=True, closes=True):
+            if i % BANK_SLOTS == 0 and opens:
                 new_sums = sums_pool.tile([P, BANK_SLOTS, OUT], F32, name="sums_tile")
                 sums[i // BANK_SLOTS] = new_sums
             for r in range(first, end):
@@ -185,8 +185,8 @@ def tile_testmmrsmodel_t_kernel(tc, hidden_states_bytes, hidden_states_scale, ga
                     lhsT_scale=block_scales[i][:, cols],
                     rhs=w_codes[:].bitcast(FP8X4),
                     rhs_scale=w_block_scales[:],
-                    start=(r == 0),
-                    stop=(r == CHUNKS - 1),
+                    start=(opens and r == first),
+                    stop=(closes and r == end - 1),
                 )
 
         def turn_gate_proj():
@@ -231,11 +231,9 @@ def tile_testmmrsmodel_t_kernel(tc, hidden_states_bytes, hidden_states_scale, ga
                     turn(step + 1, b)
             if step - 1 == SLOTS - 1:
                 store(SLOTS - BANK_SLOTS, BANK_SLOTS - 1)
-                first = 0
-                for n_units in LAST_PIECES:
-                    quantize(step - 1, first, first + n_units)
-                    multiply(step - 1, first, first + n_units)
-                    first += n_units
+                for first, end in LAST_PIECES:
+                    quantize(step - 1, first, end)
+                    multiply(step - 1, first, end, opens=(first, end) == LAST_PIECES[0], closes=(first, end) == LAST_PIECES[-1])
                 store(SLOTS - 1, 1)
             elif is_slot(step - 1):
                 multiply(step - 1, 0, CHUNKS)

@@ -74,12 +74,6 @@ def tile_testmmrsmodel_t_kernel(tc, hidden_states_bytes, hidden_states_scale, ga
         nc.gpsimd.memset(warm_in[:], 0.0)
         nc.scalar.copy(out=warm_out[:], in_=warm_in[:])
 
-        scale_pair = keep.tile([P, PAIR_COLS * PACK], F32, name="scale_pair")
-        nc.vector.tensor_copy(
-            out=scale_pair[:].rearrange("p (m t) -> p m t", t=PACK),
-            in_=scale_cols[:].unsqueeze(1).to_broadcast([P, PAIR_COLS, PACK]),
-        )
-
         w_grouped = keep.tile([P, K], BF16, name="w_grouped", align_bytes=64)
         w_codes = keep.tile([P, OUT], U32, name="w_codes", align_bytes=64)
         w_block_scales = keep.tile([P, OUT], U8, name="w_block_scales", align_bytes=64)
@@ -129,7 +123,7 @@ def tile_testmmrsmodel_t_kernel(tc, hidden_states_bytes, hidden_states_scale, ga
             nc.vector.tensor_tensor(
                 out=pair_of_grouped(i, b).rearrange("p (m u e) -> p m u e", u=2, e=2),
                 in0=halves_of(i, b).rearrange("p (u m e) -> p m u e", u=2, e=2),
-                in1=scale_pair[:].rearrange("p (m u e) -> p m u e", u=2, e=2),
+                in1=scale_cols[:].rearrange("p (u e) -> p u e", e=2).unsqueeze(1).to_broadcast([P, PAIR_COLS, 2, 2]),
                 op=mybir.AluOpType.mult,
             )
 

@@ -198,7 +198,7 @@ def tile_testmmrsmodel_t_kernel(tc, hidden_states_bytes, hidden_states_scale, ga
                 for b in range(scalar_pairs(step)):
                     scalar_product(step, b)
                 vector_product(step, scalar_pairs(step))
-            if step == 0:
+            if step == 1:
                 nc.vector.quantize_mx(out=w_codes[:].bitcast(FP8X4), scales=w_block_scales[:], in_=w_grouped[:])
             if is_slot(step - 1) and step - 1 != SLOTS - 1:
                 quantize(step - 1, 0, CHUNKS)

@@ -110,10 +110,12 @@ def tile_testmmrsmodel_t_kernel(tc, hidden_states_bytes, hidden_states_scale, ga
         def turn(i, b):
             words = widened[i][:].bitcast(F32)
             bank = turned_pool.tile([P, 2, 2, P], F32, name="bank")
+            woven_bank = bank[:].rearrange("p a b c -> p (a b c)").rearrange("p (n c u) -> p u n c", n=2, u=2)
             for n in range(2):
                 word0 = WORDS * (2 * b + n)
                 for u in range(2):
-                    nc.tensor.transpose(bank[:, u, n, :], words[:, word0 + u : word0 + WORDS : 2], ident[:])
+                    target = bank[:, u, n, :] if b < scalar_pairs(i) else woven_bank[:, u, n, :]
+                    nc.tensor.transpose(target, words[:, word0 + u : word0 + WORDS : 2], ident[:])
             banks[(i, b)] = bank
 
         def halves_of(i, b):
@@ -121,9 +123,9 @@ def tile_testmmrsmodel_t_kernel(tc, hidden_states_bytes, hidden_states_scale, ga
 
         def vector_product(i, b):
             nc.vector.tensor_tensor(
-                out=pair_of_grouped(i, b).rearrange("p (m u e) -> p m u e", u=2, e=2),
-                in0=halves_of(i, b).rearrange("p (u m e) -> p m u e", u=2, e=2),
-                in1=scale_cols[:].rearrange("p (u e) -> p u e", e=2).unsqueeze(1).to_broadcast([P, PAIR_COLS, 2, 2]),
+                out=pair_of_grouped(i, b).rearrange("p (m t) -> p m t", t=PACK),
+                in0=halves_of(i, b).rearrange("p (m t) -> p m t", t=PACK),
+                in1=scale_cols[:].unsqueeze(1).to_broadcast([P, PAIR_COLS, PACK]),
                 op=mybir.AluOpType.mult,
             )
 

@@ -109,22 +109,20 @@ def tile_testmmrsmodel_t_kernel(tc, hidden_states_bytes, hidden_states_scale, ga
 
         def turn(i, b):
             words = widened[i][:].bitcast(F32)
-            bank = turned_pool.tile([P, 2, 2, P], F32, name="bank")
-            woven_bank = bank[:].rearrange("p a b c -> p (a b c)").rearrange("p (n c u) -> p u n c", n=2, u=2)
+            bank = turned_pool.tile([P, 2, P, 2], F32, name="bank")
             for n in range(2):
                 word0 = WORDS * (2 * b + n)
                 for u in range(2):
-                    target = bank[:, u, n, :] if b < scalar_pairs(i) else woven_bank[:, u, n, :]
-                    nc.tensor.transpose(target, words[:, word0 + u : word0 + WORDS : 2], ident[:])
+                    nc.tensor.transpose(bank[:, n, :, u], words[:, word0 + u : word0 + WORDS : 2], ident[:])
             banks[(i, b)] = bank
 
         def halves_of(i, b):
-            return banks[(i, b)][:].rearrange("p u n c -> p (u n c)").bitcast(BF16)
+            return banks[(i, b)][:].rearrange("p n c u -> p (n c u)").bitcast(BF16).rearrange("p (m t) -> p m t", t=PACK)
 
         def vector_product(i, b):
             nc.vector.tensor_tensor(
                 out=pair_of_grouped(i, b).rearrange("p (m t) -> p m t", t=PACK),
-                in0=halves_of(i, b).rearrange("p (m t) -> p m t", t=PACK),
+                in0=halves_of(i, b),
                 in1=scale_cols[:].unsqueeze(1).to_broadcast([P, PAIR_COLS, PACK]),
                 op=mybir.AluOpType.mult,
             )
@@ -132,11 +130,10 @@ def tile_testmmrsmodel_t_kernel(tc, hidden_states_bytes, hidden_states_scale, ga
         def scalar_product(i, b):
             new_planes = short.tile([P, PACK, PAIR_COLS], BF16, name="planes_tile%d" % b)
             planes[(i, b)] = new_planes
-            halves = halves_of(i, b).rearrange("p (u m e) -> p u m e", u=2, e=2)
             for t in range(PACK):
                 nc.scalar.activation(
                     out=new_planes[:, t, :],
-                    in_=halves[:, t // 2, :, t % 2],
+                    in_=halves_of(i, b)[:, :, t],
                     func=mybir.ActivationFunctionType.Copy,
                     scale=scale_cols[:, t : t + 1],
                 )
@@ -187,13 +184,10 @@ def tile_testmmrsmodel_t_kernel(tc, hidden_states_bytes, hidden_states_scale, ga
 
         def turn_gate_proj():
             w_words = w_rows[:].bitcast(F32)
-            w_bank = turned_pool.tile([P, 2, 2, P], F32, name="bank")
+            w_bank = turned_pool.tile([P, 2, P, 2], F32, name="bank")
             for u in range(2):
-                nc.tensor.transpose(w_bank[:, u, 0, :], w_words[:, u:WORDS:2], ident[:])
-            nc.scalar.copy(
-                out=w_grouped[:].bitcast(F32).rearrange("p (c u) -> p c u", u=2),
-                in_=w_bank[:, :, 0, :].rearrange("p u c -> p c u"),
-            )
+                nc.tensor.transpose(w_bank[:, 0, :, u], w_words[:, u:WORDS:2], ident[:])
+            nc.scalar.copy(out=w_grouped[:].bitcast(F32), in_=w_bank[:, 0, :, :].rearrange("p c u -> p (c u)"))
 
         for step in range(-2, SLOTS + 2):
             if is_slot(step):

@@ -36,8 +36,12 @@ def scalar_pairs(i):
     return 2 if i >= SLOTS - 2 else 1
 
 
+def scalar_part(i):
+    return 0 if i >= SLOTS - 2 else 32
+
+
 def scalar_widens(i):
-    return 7 * K // 2
+    return 13 * K // 4
 
 
 def tile_testmmrsmodel_t_kernel(tc, hidden_states_bytes, hidden_states_scale, gate_proj, world_size, out):
@@ -119,29 +123,29 @@ def tile_testmmrsmodel_t_kernel(tc, hidden_states_bytes, hidden_states_scale, ga
         def halves_of(i, b):
             return banks[(i, b)][:].rearrange("p n c u -> p (n c u)").bitcast(BF16).rearrange("p (m t) -> p m t", t=PACK)
 
-        def vector_product(i, b):
+        def vector_product(i, b, first_col=0):
             nc.vector.tensor_tensor(
-                out=pair_of_grouped(i, b).rearrange("p (m t) -> p m t", t=PACK),
-                in0=halves_of(i, b),
-                in1=scale_cols[:].unsqueeze(1).to_broadcast([P, PAIR_COLS, PACK]),
+                out=pair_of_grouped(i, b).rearrange("p (m t) -> p m t", t=PACK)[:, first_col:, :],
+                in0=halves_of(i, b)[:, first_col:, :],
+                in1=scale_cols[:].unsqueeze(1).to_broadcast([P, PAIR_COLS - first_col, PACK]),
                 op=mybir.AluOpType.mult,
             )
 
-        def scalar_product(i, b):
-            new_planes = short.tile([P, PACK, PAIR_COLS], BF16, name="planes_tile%d" % b)
+        def scalar_product(i, b, n_cols=PAIR_COLS):
+            new_planes = short.tile([P, PACK, n_cols], BF16, name="planes_tile%d" % b)
             planes[(i, b)] = new_planes
             for t in range(PACK):
                 nc.scalar.activation(
                     out=new_planes[:, t, :],
-                    in_=halves_of(i, b)[:, :, t],
+                    in_=halves_of(i, b)[:, 0:n_cols, t],
                     func=mybir.ActivationFunctionType.Copy,
                     scale=scale_cols[:, t : t + 1],
                 )
 
-        def weave(i, b):
-            woven = pair_of_grouped(i, b).rearrange("p (m t) -> p m t", t=PACK)
+        def weave(i, b, n_cols=PAIR_COLS):
+            woven = pair_of_grouped(i, b)[:, 0 : n_cols * PACK].rearrange("p (m t) -> p m t", t=PACK)
             by_column = planes[(i, b)][:].rearrange("p t m -> p m t")
-            if b == GPSIMD_WEAVES_PAIR:
+            if b == GPSIMD_WEAVES_PAIR and n_cols == PAIR_COLS:
                 nc.gpsimd.tensor_scalar(
                     out=woven, in0=by_column, scalar1=1.0, scalar2=0.0, op0=mybir.AluOpType.mult, op1=mybir.AluOpType.add
                 )
@@ -190,21 +194,34 @@ def tile_testmmrsmodel_t_kernel(tc, hidden_states_bytes, hidden_states_scale, ga
             nc.scalar.copy(out=w_grouped[:].bitcast(F32), in_=w_bank[:, 0, :, :].rearrange("p c u -> p (c u)"))
 
         for step in range(-2, SLOTS + 2):
+            whole = scalar_pairs(step)
+            part = scalar_part(step)
             if is_slot(step):
-                for b in range(scalar_pairs(step)):
+                if part and step == 0:
+                    scalar_product(step, whole, part)
+                for b in range(whole):
                     scalar_product(step, b)
-                vector_product(step, scalar_pairs(step))
+                if part:
+                    vector_product(step, whole + 1)
+                vector_product(step, whole, part)
             if step == 1:
                 nc.vector.quantize_mx(out=w_codes[:].bitcast(FP8X4), scales=w_block_scales[:], in_=w_grouped[:])
             if is_slot(step - 1) and step - 1 != SLOTS - 1:
                 quantize(step - 1, 0, CHUNKS)
             if is_slot(step):
-                for b in range(scalar_pairs(step) + 1, PAIRS):
+                for b in range(whole + (2 if part else 1), PAIRS):
                     vector_product(step, b)
-                for b in range(scalar_pairs(step)):
+                for b in range(whole):
                     weave(step, b)
+                if part:
+                    weave(step, whole, part)
             if is_slot(step - 2) and (step - 2) % BANK_SLOTS == BANK_SLOTS - 1 and step - 2 != SLOTS - 1:
                 store(step - 2 - (BANK_SLOTS - 1), BANK_SLOTS)
+            if is_slot(step + 1):
+                for b in range(PAIRS):
+                    turn(step + 1, b)
+                if scalar_part(step + 1) and step + 1 > 0:
+                    scalar_product(step + 1, scalar_pairs(step + 1), scalar_part(step + 1))
             if step + 2 == 0:
                 widen(nc.scalar.copy, 0, 0, 2)
                 for b in range(1, PAIRS):
@@ -216,9 +233,6 @@ def tile_testmmrsmodel_t_kernel(tc, hidden_states_bytes, hidden_states_scale, ga
                 middle = (split + CHUNKS * K) // 2
                 widen_columns(nc.gpsimd.tensor_copy, step + 2, split, middle)
                 widen_columns(nc.gpsimd.tensor_copy, step + 2, middle, CHUNKS * K)
-            if is_slot(step + 1):
-                for b in range(PAIRS):
-                    turn(step + 1, b)
             if step - 1 == SLOTS - 1:
                 store(SLOTS - BANK_SLOTS, BANK_SLOTS - 1)
                 for first, end in LAST_PIECES:

@@ -230,9 +230,12 @@ def tile_testmmrsmodel_t_kernel(tc, hidden_states_bytes, hidden_states_scale, ga
             elif is_slot(step + 2):
                 split = scalar_widens(step + 2)
                 widen_columns(nc.scalar.copy, step + 2, 0, split)
-                middle = (split + CHUNKS * K) // 2
-                widen_columns(nc.gpsimd.tensor_copy, step + 2, split, middle)
-                widen_columns(nc.gpsimd.tensor_copy, step + 2, middle, CHUNKS * K)
+                if step + 2 <= 2:
+                    middle = (split + CHUNKS * K) // 2
+                    widen_columns(nc.gpsimd.tensor_copy, step + 2, split, middle)
+                    widen_columns(nc.gpsimd.tensor_copy, step + 2, middle, CHUNKS * K)
+                else:
+                    widen_columns(nc.gpsimd.tensor_copy, step + 2, split, CHUNKS * K)
             if step - 1 == SLOTS - 1:
                 store(SLOTS - BANK_SLOTS, BANK_SLOTS - 1)
                 for first, end in LAST_PIECES:

@@ -37,11 +37,11 @@ def scalar_pairs(i):
 
 
 def scalar_part(i):
-    return 0 if i >= SLOTS - 2 else 32
+    return 0 if i >= SLOTS - 2 else 56
 
 
 def scalar_widens(i):
-    return 13 * K // 4
+    return 3 * K
 
 
 def tile_testmmrsmodel_t_kernel(tc, hidden_states_bytes, hidden_states_scale, gate_proj, world_size, out):

@@ -23,7 +23,7 @@ PAIRS = CHUNKS // 2
 PAIR_COLS = 2 * P
 LAST_PIECES = [(4, 8), (0, 2), (2, 4)]
 
-GPSIMD_WEAVES_PAIR = 1
+GPSIMD_WEAVES_PAIR = 0
 
 FLOPS = 2 * CHUNKS * ROWS * K * OUT
 
@@ -145,7 +145,7 @@ def tile_testmmrsmodel_t_kernel(tc, hidden_states_bytes, hidden_states_scale, ga
         def weave(i, b, n_cols=PAIR_COLS):
             woven = pair_of_grouped(i, b)[:, 0 : n_cols * PACK].rearrange("p (m t) -> p m t", t=PACK)
             by_column = planes[(i, b)][:].rearrange("p t m -> p m t")
-            if b == GPSIMD_WEAVES_PAIR and n_cols == PAIR_COLS:
+            if scalar_pairs(i) == 2 and b == GPSIMD_WEAVES_PAIR:
                 nc.gpsimd.tensor_scalar(
                     out=woven, in0=by_column, scalar1=1.0, scalar2=0.0, op0=mybir.AluOpType.mult, op1=mybir.AluOpType.add
                 )

@@ -23,6 +23,8 @@ PAIRS = CHUNKS // 2
 PAIR_COLS = 2 * P
 LAST_PIECES = [(4, 8), (0, 2), (2, 4)]
 
+SCALE_COPIES = 8
+
 GPSIMD_WEAVES_PAIR = 0
 
 FLOPS = 2 * CHUNKS * ROWS * K * OUT
@@ -71,6 +73,11 @@ def tile_testmmrsmodel_t_kernel(tc, hidden_states_bytes, hidden_states_scale, ga
                 nc.sync.dma_start(out=slot_bytes[:, r : r + units, :], in_=bytes_by_slot[i][:, r : r + units, :])
             x_bytes.append(slot_bytes)
 
+        scale_run = keep.tile([P, SCALE_COPIES * PACK], F32, name="scale_run")
+        nc.vector.tensor_copy(
+            out=scale_run[:].rearrange("p (m t) -> p m t", t=PACK),
+            in_=scale_cols[:].unsqueeze(1).to_broadcast([P, SCALE_COPIES, PACK]),
+        )
         ident = keep.tile([P, P], F32, name="ident")
         make_identity(nc, ident[:])
         warm_in = keep.tile([P, 1], F32, name="warm_in")
@@ -124,10 +131,11 @@ def tile_testmmrsmodel_t_kernel(tc, hidden_states_bytes, hidden_states_scale, ga
             return banks[(i, b)][:].rearrange("p n c u -> p (n c u)").bitcast(BF16).rearrange("p (m t) -> p m t", t=PACK)
 
         def vector_product(i, b, first_col=0):
+            run = SCALE_COPIES * PACK
             nc.vector.tensor_tensor(
-                out=pair_of_grouped(i, b).rearrange("p (m t) -> p m t", t=PACK)[:, first_col:, :],
-                in0=halves_of(i, b)[:, first_col:, :],
-                in1=scale_cols[:].unsqueeze(1).to_broadcast([P, PAIR_COLS - first_col, PACK]),
+                out=pair_of_grouped(i, b)[:, first_col * PACK :].rearrange("p (g e) -> p g e", e=run),
+                in0=halves_of(i, b)[:, first_col:, :].rearrange("p (g m) t -> p g (m t)", m=SCALE_COPIES),
+                in1=scale_run[:].unsqueeze(1).to_broadcast([P, (PAIR_COLS - first_col) // SCALE_COPIES, run]),
                 op=mybir.AluOpType.mult,
             )
 

@@ -209,14 +209,14 @@ def tile_testmmrsmodel_t_kernel(tc, hidden_states_bytes, hidden_states_scale, ga
                     scalar_product(step, whole, part)
                 for b in range(whole):
                     scalar_product(step, b)
-                if part:
-                    vector_product(step, whole + 1)
-                vector_product(step, whole, part)
+                vector_product(step, whole + 1 if part else whole)
             if step == 1:
                 nc.vector.quantize_mx(out=w_codes[:].bitcast(FP8X4), scales=w_block_scales[:], in_=w_grouped[:])
             if is_slot(step - 1) and step - 1 != SLOTS - 1:
                 quantize(step - 1, 0, CHUNKS)
             if is_slot(step):
+                if part:
+                    vector_product(step, whole, part)
                 for b in range(whole + (2 if part else 1), PAIRS):
                     vector_product(step, b)
                 for b in range(whole):

from contextlib import ExitStack

import concourse.mybir as mybir
from concourse.masks import make_identity

F32 = mybir.dt.float32
BF16 = mybir.dt.bfloat16
U32 = mybir.dt.uint32
U8 = mybir.dt.uint8
FP8 = mybir.dt.float8_e4m3fn
FP8X4 = mybir.dt.float8_e4m3fn_x4

P = 128
CHUNKS = 8
ROWS = 2048
K = 512
OUT = 128
SLOTS = ROWS // P
PACK = 4
WORDS = K // 2
BANK_SLOTS = 4
PAIRS = CHUNKS // 2
PAIR_COLS = 2 * P
LAST_PIECES = [(4, 8), (0, 2), (2, 4)]

SCALE_COPIES = 8

GPSIMD_WEAVES_PAIR = 0

FLOPS = 2 * CHUNKS * ROWS * K * OUT


def is_slot(i):
    return 0 <= i < SLOTS


def scalar_pairs(i):
    return 2 if i >= SLOTS - 2 else 1


def scalar_part(i):
    return 0 if i >= SLOTS - 2 else 56


def scalar_widens(i):
    return 3 * K


def tile_testmmrsmodel_t_kernel(tc, hidden_states_bytes, hidden_states_scale, gate_proj, world_size, out):
    nc = tc.nc
    assert world_size == CHUNKS

    bytes_by_slot = hidden_states_bytes.rearrange("r (p i) k -> i p r k", i=SLOTS)
    out_by_slot = out.rearrange("(p i) o -> p i o", i=SLOTS)

    with ExitStack() as ctx:
        ctx.enter_context(tc.manual_schedule())
        keep = ctx.enter_context(tc.tile_pool(name="keep", bufs=1))
        short = ctx.enter_context(tc.tile_pool(name="short", bufs=3))
        rows_pool = ctx.enter_context(tc.tile_pool(name="rows_pool", bufs=3))
        turned_pool = ctx.enter_context(tc.psum_pool(name="turned_pool", bufs=6))
        sums_pool = ctx.enter_context(tc.psum_pool(name="sums_pool", bufs=2))

        w_rows = keep.tile([P, K], BF16, name="w_rows")
        scale_cols = keep.tile([P, PACK], F32, name="scale_cols")
        nc.scalar.dma_start(out=scale_cols[:], in_=hidden_states_scale.rearrange("a b (p t) -> p (a b t)", t=PACK))
        nc.scalar.dma_start(out=w_rows[:], in_=gate_proj)
        x_bytes = []
        for i in range(SLOTS):
            slot_bytes = keep.tile([P, CHUNKS, K], U8, name="x_bytes%d" % i)
            units = 2 if i == 0 else 4
            for r in range(0, CHUNKS, units):
                nc.sync.dma_start(out=slot_bytes[:, r : r + units, :], in_=bytes_by_slot[i][:, r : r + units, :])
            x_bytes.append(slot_bytes)

        scale_run = keep.tile([P, SCALE_COPIES * PACK], F32, name="scale_run")
        nc.vector.tensor_copy(
            out=scale_run[:].rearrange("p (m t) -> p m t", t=PACK),
            in_=scale_cols[:].unsqueeze(1).to_broadcast([P, SCALE_COPIES, PACK]),
        )
        ident = keep.tile([P, P], F32, name="ident")
        make_identity(nc, ident[:])
        warm_in = keep.tile([P, 1], F32, name="warm_in")
        warm_out = keep.tile([P, 1], F32, name="warm_out")
        nc.gpsimd.memset(warm_in[:], 0.0)
        nc.scalar.copy(out=warm_out[:], in_=warm_in[:])

        w_grouped = keep.tile([P, K], BF16, name="w_grouped", align_bytes=64)
        w_codes = keep.tile([P, OUT], U32, name="w_codes", align_bytes=64)
        w_block_scales = keep.tile([P, OUT], U8, name="w_block_scales", align_bytes=64)

        widened = {}
        banks = {}
        planes = {}
        grouped = {}
        codes = {}
        block_scales = {}
        sums = {}

        def as_fp8(i):
            return x_bytes[i][:].rearrange("p r k -> p (r k)").bitcast(FP8)

        def grouped_of(i):
            if i not in grouped:
                new_grouped = rows_pool.tile([P, CHUNKS * K], BF16, name="rows_tile", align_bytes=64)
                grouped[i] = new_grouped
            return grouped[i]

        def pair_of_grouped(i, b):
            return grouped_of(i)[:, 2 * b * K : (2 * b + 2) * K]

        def widen_columns(engine_copy, i, first_col, end_col):
            if i not in widened:
                new_widened = rows_pool.tile([P, CHUNKS * K], BF16, name="rows_tile", align_bytes=64)
                widened[i] = new_widened
            engine_copy(out=widened[i][:, first_col:end_col], in_=as_fp8(i)[:, first_col:end_col])

        def widen(engine_copy, i, first, end):
            widen_columns(engine_copy, i, first * K, end * K)

        def turn(i, b):
            words = widened[i][:].bitcast(F32)
            bank = turned_pool.tile([P, 2, P, 2], F32, name="bank")
            for n in range(2):
                word0 = WORDS * (2 * b + n)
                for u in range(2):
                    nc.tensor.transpose(bank[:, n, :, u], words[:, word0 + u : word0 + WORDS : 2], ident[:])
            banks[(i, b)] = bank

        def halves_of(i, b):
            return banks[(i, b)][:].rearrange("p n c u -> p (n c u)").bitcast(BF16).rearrange("p (m t) -> p m t", t=PACK)

        def vector_product(i, b, first_col=0):
            run = SCALE_COPIES * PACK
            nc.vector.tensor_tensor(
                out=pair_of_grouped(i, b)[:, first_col * PACK :].rearrange("p (g e) -> p g e", e=run),
                in0=halves_of(i, b)[:, first_col:, :].rearrange("p (g m) t -> p g (m t)", m=SCALE_COPIES),
                in1=scale_run[:].unsqueeze(1).to_broadcast([P, (PAIR_COLS - first_col) // SCALE_COPIES, run]),
                op=mybir.AluOpType.mult,
            )

        def scalar_product(i, b, n_cols=PAIR_COLS):
            new_planes = short.tile([P, PACK, n_cols], BF16, name="planes_tile%d" % b)
            planes[(i, b)] = new_planes
            for t in range(PACK):
                nc.scalar.activation(
                    out=new_planes[:, t, :],
                    in_=halves_of(i, b)[:, 0:n_cols, t],
                    func=mybir.ActivationFunctionType.Copy,
                    scale=scale_cols[:, t : t + 1],
                )

        def weave(i, b, n_cols=PAIR_COLS):
            woven = pair_of_grouped(i, b)[:, 0 : n_cols * PACK].rearrange("p (m t) -> p m t", t=PACK)
            by_column = planes[(i, b)][:].rearrange("p t m -> p m t")
            if scalar_pairs(i) == 2 and b == GPSIMD_WEAVES_PAIR:
                nc.gpsimd.tensor_scalar(
                    out=woven, in0=by_column, scalar1=1.0, scalar2=0.0, op0=mybir.AluOpType.mult, op1=mybir.AluOpType.add
                )
            else:
                nc.scalar.copy(out=woven, in_=by_column)

        def quantize(i, first, end):
            if i not in codes:
                new_codes = short.tile([P, CHUNKS * P], U32, name="codes_tile", align_bytes=64)
                new_block_scales = short.tile([P, CHUNKS * P], U8, name="block_scales_tile", align_bytes=64)
                codes[i] = new_codes
                block_scales[i] = new_block_scales
            nc.vector.quantize_mx(
                out=codes[i][:, first * P : end * P].bitcast(FP8X4),
                scales=block_scales[i][:, first * P : end * P],
                in_=grouped[i][:, first * K : end * K],
            )

        def store(first_slot, n_slots):
            place = first_slot % BANK_SLOTS
            result = short.tile([P, BANK_SLOTS, OUT], F32, name="result")
            nc.scalar.copy(out=result[:, 0:n_slots, :], in_=sums[first_slot // BANK_SLOTS][:, place : place + n_slots, :])
            nc.sync.dma_start(out=out_by_slot[:, first_slot : first_slot + n_slots, :], in_=result[:, 0:n_slots, :])

        def multiply(i, first, end, opens=True, closes=True):
            if i % BANK_SLOTS == 0 and opens:
                new_sums = sums_pool.tile([P, BANK_SLOTS, OUT], F32, name="sums_tile")
                sums[i // BANK_SLOTS] = new_sums
            for r in range(first, end):
                cols = slice(r * P, (r + 1) * P)
                nc.tensor.matmul_mx(
                    out=sums[i // BANK_SLOTS][:, i % BANK_SLOTS, :],
                    lhsT=codes[i][:, cols].bitcast(FP8X4),
                    lhsT_scale=block_scales[i][:, cols],
                    rhs=w_codes[:].bitcast(FP8X4),
                    rhs_scale=w_block_scales[:],
                    start=(opens and r == first),
                    stop=(closes and r == end - 1),
                )

        def turn_gate_proj():
            w_words = w_rows[:].bitcast(F32)
            w_bank = turned_pool.tile([P, 2, P, 2], F32, name="bank")
            for u in range(2):
                nc.tensor.transpose(w_bank[:, 0, :, u], w_words[:, u:WORDS:2], ident[:])
            nc.scalar.copy(out=w_grouped[:].bitcast(F32), in_=w_bank[:, 0, :, :].rearrange("p c u -> p (c u)"))

        for step in range(-2, SLOTS + 2):
            whole = scalar_pairs(step)
            part = scalar_part(step)
            if is_slot(step):
                if part and step == 0:
                    scalar_product(step, whole, part)
                for b in range(whole):
                    scalar_product(step, b)
                vector_product(step, whole + 1 if part else whole)
            if step == 1:
                nc.vector.quantize_mx(out=w_codes[:].bitcast(FP8X4), scales=w_block_scales[:], in_=w_grouped[:])
            if is_slot(step - 1) and step - 1 != SLOTS - 1:
                quantize(step - 1, 0, CHUNKS)
            if is_slot(step):
                if part:
                    vector_product(step, whole, part)
                for b in range(whole + (2 if part else 1), PAIRS):
                    vector_product(step, b)
                for b in range(whole):
                    weave(step, b)
                if part:
                    weave(step, whole, part)
            if is_slot(step - 2) and (step - 2) % BANK_SLOTS == BANK_SLOTS - 1 and step - 2 != SLOTS - 1:
                store(step - 2 - (BANK_SLOTS - 1), BANK_SLOTS)
            if is_slot(step + 1):
                for b in range(PAIRS):
                    turn(step + 1, b)
                if scalar_part(step + 1) and step + 1 > 0:
                    scalar_product(step + 1, scalar_pairs(step + 1), scalar_part(step + 1))
            if step + 2 == 0:
                widen(nc.scalar.copy, 0, 0, 2)
                for b in range(1, PAIRS):
                    widen(nc.vector.tensor_copy, 0, 2 * b, 2 * b + 2)
                turn_gate_proj()
            elif is_slot(step + 2):
                split = scalar_widens(step + 2)
                widen_columns(nc.scalar.copy, step + 2, 0, split)
                if step + 2 <= 2:
                    middle = (split + CHUNKS * K) // 2
                    widen_columns(nc.gpsimd.tensor_copy, step + 2, split, middle)
                    widen_columns(nc.gpsimd.tensor_copy, step + 2, middle, CHUNKS * K)
                else:
                    widen_columns(nc.gpsimd.tensor_copy, step + 2, split, CHUNKS * K)
            if step - 1 == SLOTS - 1:
                store(SLOTS - BANK_SLOTS, BANK_SLOTS - 1)
                for first, end in LAST_PIECES:
                    quantize(step - 1, first, end)
                    multiply(step - 1, first, end, opens=(first, end) == LAST_PIECES[0], closes=(first, end) == LAST_PIECES[-1])
                store(SLOTS - 1, 1)
            elif is_slot(step - 1):
                multiply(step - 1, 0, CHUNKS)
